import numpy as np
import ml_dtypes


def mxq(x, axis, fmt="e4m3"):
    dtype, down = {"e4m3": (ml_dtypes.float8_e4m3fn, 7), "e5m2": (ml_dtypes.float8_e5m2, 14)}[fmt]
    v = np.moveaxis(np.asarray(x, np.float32).astype(ml_dtypes.bfloat16).astype(np.float64), axis, -1)
    blocks = v.reshape(v.shape[:-1] + (-1, 32))
    amax = np.abs(blocks).max(-1, keepdims=True)
    byte = np.maximum(np.where(amax > 0, np.frexp(amax)[1] - 1 + 127, 0) - down, 1)
    scale = np.exp2(byte - 127.0)
    codes = (blocks / scale).astype(np.float32).astype(dtype).astype(np.float64)
    return np.moveaxis((codes * scale).reshape(v.shape), -1, axis)


WIDE = False


def mx_kscale(k):
    if not WIDE:
        return np.ones(k)
    levels = np.array([10, -10, 5, -5, 0])
    a = np.random.permutation(np.resize(levels, k // 512 * 4)).reshape(k // 512, 4)
    idx = np.arange(k)
    return np.exp2(a[idx // 512, idx % 128 // 32])


BF16 = ml_dtypes.bfloat16


def bf(x):
    return np.asarray(x, np.float32).astype(BF16)


def f64(x):
    return np.asarray(x).astype(np.float64)


B, P, K, D, L, C0, C1, C2, C3 = 1024, 64, 128, 256, 4, 64, 128, 256, 512
C = C3
F = 2 * C
EPS = 1e-5


def layernorm(x, g, b):
    m = x.mean(axis=-1, keepdims=True)
    v = x.var(axis=-1, keepdims=True)
    return (x - m) / np.sqrt(v + EPS) * g + b


def l2norm(x):
    n = np.sqrt((x * x).sum(axis=-1, keepdims=True))
    return x / np.maximum(n, 1e-12)


def setup_inputs():
    s = mx_kscale(F)
    return {"pooled": bf(0.5 + 2.0 * np.random.standard_normal((B, C))),
            "proto": bf(np.random.standard_normal((1, C)) + np.random.standard_normal((P, C))),
            "ln_g": bf((1.0 + 0.1 * np.random.standard_normal(F)) * s),
            "ln_b": bf(0.1 * np.random.standard_normal(F) * s),
            "W": bf(np.random.standard_normal((F, D)) / np.sqrt(F) / s[:, None]),
            "b": bf(0.1 * np.random.standard_normal(D))}


def reference(pooled, proto, ln_g, ln_b, W, b):
    pl = f64(pooled)
    proto_ctx = np.broadcast_to(f64(proto).mean(axis=0, keepdims=True), pl.shape)
    fused = np.concatenate([pl, proto_ctx], axis=1)
    z = layernorm(fused, f64(ln_g), f64(ln_b))
    h = np.maximum((mxq(z, 1, "e4m3") @ mxq(f64(W), 0, "e4m3")) + f64(b), 0.0)
    return l2norm(h)

@@ -1,0 +1,201 @@
+from contextlib import ExitStack
+
+import concourse.mybir as mybir
+from concourse.masks import make_identity
+
+F32 = mybir.dt.float32
+BF16 = mybir.dt.bfloat16
+U32 = mybir.dt.uint32
+U8 = mybir.dt.uint8
+FP8X4 = mybir.dt.float8_e4m3fn_x4
+ALU = mybir.AluOpType
+ACT = mybir.ActivationFunctionType
+
+P = 128
+PACK = 4
+ROWS = 1024
+C = 512
+HALVES = 2
+D = 256
+PROTOS = 64
+TILES = ROWS // P
+GROUP = 2
+GROUPS = TILES // GROUP
+PAIR = 2
+K_BLOCKS = HALVES * PACK
+STATS = 6
+EPS = 1e-5
+FLOPS = 2 * ROWS * HALVES * C * D
+
+
+def tile_textguidedcamfusion_pa_s_kernel(tc, pooled, proto, ln_g, ln_b, W, b, out):
+    nc = tc.nc
+    with ExitStack() as ctx:
+        keep = ctx.enter_context(tc.tile_pool(name="keep", bufs=1))
+        scratch = ctx.enter_context(tc.tile_pool(name="scratch", bufs=2))
+        banks = ctx.enter_context(tc.psum_pool(name="banks", bufs=6))
+        products = ctx.enter_context(tc.psum_pool(name="products", bufs=2))
+
+        x = keep.tile([P, TILES, C], BF16)
+        pooled_rows = pooled.rearrange("(p j) c -> p j c", j=TILES)
+        out_rows = out.rearrange("(p j) d -> p j d", j=TILES)
+        w_raw = keep.tile([P, K_BLOCKS, D], BF16)
+        nc.sync.dma_start(out=x[:, 0:GROUP, :], in_=pooled_rows[:, 0:GROUP, :])
+        nc.sync.dma_start(out=x[:, GROUP : 2 * GROUP, :], in_=pooled_rows[:, GROUP : 2 * GROUP, :])
+        nc.sync.dma_start(out=w_raw[:], in_=W.rearrange("(kb p) d -> p kb d", p=P))
+        nc.sync.dma_start(out=x[:, 2 * GROUP : TILES, :], in_=pooled_rows[:, 2 * GROUP : TILES, :])
+
+        proto_pad = keep.tile([P, C], BF16)
+        nc.vector.memset(proto_pad[PROTOS:P, :], 0.0)
+        nc.scalar.dma_start(out=proto_pad[0:PROTOS, :], in_=proto)
+        gain_rows = keep.tile([P, P], BF16)
+        nc.vector.memset(gain_rows[:], 0.0)
+        nc.scalar.dma_start(out=gain_rows[0:K_BLOCKS, :], in_=ln_g.rearrange("(r c) -> r c", c=P))
+        nc.scalar.dma_start(out=gain_rows[K_BLOCKS : 2 * K_BLOCKS, :], in_=ln_b.rearrange("(r c) -> r c", c=P))
+        bias_pad = keep.tile([P, D], BF16)
+        nc.vector.memset(bias_pad[:], 0.0)
+        nc.scalar.dma_start(out=bias_pad[0:1, :], in_=b.rearrange("(o d) -> o d", o=1))
+
+        eps_col = keep.tile([P, 1], F32)
+        nc.vector.memset(eps_col[:], EPS)
+        warm = keep.tile([P, 1], F32)
+        nc.scalar.sqrt(out=warm[:], in_=eps_col[:])
+        ones = keep.tile([P, P], BF16)
+        nc.vector.memset(ones[:], 1.0)
+        ident = keep.tile([P, P], F32)
+        make_identity(nc, ident[:])
+
+        c_sum = banks.tile([P, C], F32, tag="bank")
+        nc.tensor.matmul(out=c_sum[:], lhsT=ones[:], rhs=proto_pad[:], start=True, stop=True)
+        c_all = keep.tile([P, C], F32)
+        nc.scalar.activation(out=c_all[:], in_=c_sum[:], func=ACT.Copy, scale=1.0 / PROTOS)
+        b_sum = banks.tile([P, D], F32, tag="bank")
+        nc.tensor.matmul(out=b_sum[:], lhsT=ones[:], rhs=bias_pad[:], start=True, stop=True)
+        b_all = keep.tile([P, D], F32)
+        nc.scalar.copy(out=b_all[:], in_=b_sum[:])
+        gain_f32 = keep.tile([P, P], F32)
+        nc.vector.tensor_copy(out=gain_f32[:], in_=gain_rows[:])
+        gain_t = banks.tile([P, P], F32, tag="bank")
+        nc.tensor.transpose(gain_t[:], gain_f32[:], ident[:])
+        gain = keep.tile([P, 2 * K_BLOCKS], F32)
+        nc.vector.tensor_copy(out=gain[:], in_=gain_t[:, 0 : 2 * K_BLOCKS])
+
+        w_grouped = keep.tile([P, HALVES, D, PACK], BF16, align_bytes=64)
+        w_codes = keep.tile([P, HALVES, D], U32, align_bytes=64)
+        w_scales = keep.tile([P, HALVES, D], U8, align_bytes=64)
+        for h in range(HALVES):
+            nc.scalar.copy(
+                out=w_grouped[:, h].rearrange("p (c i) t -> p c t i", i=4),
+                in_=w_raw[:, PACK * h : PACK * (h + 1), :].rearrange("p t (c i) -> p c t i", i=4),
+            )
+        nc.vector.quantize_mx(
+            out=w_codes[:].rearrange("p h d -> p (h d)").bitcast(FP8X4),
+            scales=w_scales[:].rearrange("p h d -> p (h d)"),
+            in_=w_grouped[:].rearrange("p h d t -> p (h d t)"),
+        )
+
+        stats = keep.tile([P, TILES, HALVES, STATS], F32)
+        c_stats = keep.tile([P, STATS], F32)
+        nc.vector.bn_stats(out=c_stats[:], in_=c_all[:])
+        nc.vector.tensor_copy(out=stats[:, :, 1, :], in_=c_stats[:].unsqueeze(1).to_broadcast([P, TILES, STATS]))
+        mean_var = keep.tile([P, TILES, 2], F32)
+        std = keep.tile([P, TILES], F32)
+        rstd = keep.tile([P, TILES], F32)
+        shift = keep.tile([P, TILES], F32)
+
+        def row_statistics(g):
+            tiles = slice(GROUP * g, GROUP * (g + 1))
+            for j in range(GROUP * g, GROUP * (g + 1)):
+                nc.vector.bn_stats(out=stats[:, j, 0, :], in_=x[:, j, :])
+                nc.vector.bn_aggr(out=mean_var[:, j, :], in_=stats[:, j].rearrange("p h s -> p (h s)"))
+            nc.scalar.activation(out=std[:, tiles], in_=mean_var[:, tiles, 1], func=ACT.Sqrt, bias=eps_col[:])
+            nc.vector.reciprocal(out=rstd[:, tiles], in_=std[:, tiles])
+            nc.vector.scalar_tensor_tensor(
+                out=shift[:, tiles], in0=mean_var[:, tiles, 0], scalar=-1.0, in1=rstd[:, tiles],
+                op0=ALU.mult, op1=ALU.mult,
+            )
+
+        y = keep.tile([P, TILES, HALVES, C], F32)
+        planes = keep.tile([P, GROUPS, HALVES, PACK, GROUP * P], BF16)
+        z_grouped = keep.tile([P, GROUPS, HALVES, GROUP * P, PACK], BF16, align_bytes=64)
+        z_codes = keep.tile([P, GROUPS, HALVES, GROUP * P], U32, align_bytes=64)
+        z_scales = keep.tile([P, GROUPS, HALVES, GROUP * P], U8, align_bytes=64)
+
+        def normalise(g):
+            for j in range(GROUP * g, GROUP * (g + 1)):
+                nc.scalar.activation(
+                    out=y[:, j, 0, :], in_=x[:, j, :], func=ACT.Identity,
+                    scale=rstd[:, j : j + 1], bias=shift[:, j : j + 1],
+                )
+                nc.vector.tensor_scalar(
+                    out=y[:, j, 1, :], in0=c_all[:], scalar1=mean_var[:, j, 0:1], scalar2=rstd[:, j : j + 1],
+                    op0=ALU.subtract, op1=ALU.mult,
+                )
+
+        def quantise_z(g, h):
+            for t in range(PACK):
+                kb = PACK * h + t
+                y_t = banks.tile([P, GROUP, P], F32, tag="bank")
+                for jj in range(GROUP):
+                    nc.tensor.transpose(y_t[:, jj, :], y[:, GROUP * g + jj, h, P * t : P * (t + 1)], ident[:])
+                nc.scalar.activation(
+                    out=planes[:, g, h, t, :], in_=y_t[:].rearrange("p j m -> p (j m)"), func=ACT.Identity,
+                    scale=gain[:, kb : kb + 1], bias=gain[:, K_BLOCKS + kb : K_BLOCKS + kb + 1],
+                )
+            nc.vector.tensor_copy(
+                out=z_grouped[:, g, h].rearrange("p (c i) t -> p c t i", i=4),
+                in_=planes[:, g, h].rearrange("p t (c i) -> p c t i", i=4),
+            )
+            nc.vector.quantize_mx(
+                out=z_codes[:, g, h, :].bitcast(FP8X4),
+                scales=z_scales[:, g, h, :],
+                in_=z_grouped[:, g, h].rearrange("p r t -> p (r t)"),
+            )
+
+        pre = keep.tile([P, TILES, D], F32)
+        sumsq = keep.tile([P, TILES], F32)
+        norm = keep.tile([P, TILES], F32)
+        rnorm = keep.tile([P, TILES], F32)
+        result = keep.tile([P, TILES, D], F32)
+
+        def project(g):
+            tiles = slice(GROUP * g, GROUP * (g + 1))
+            for j0 in range(GROUP * g, GROUP * (g + 1), PAIR):
+                acc = products.tile([P, PAIR, D], F32)
+                for e in range(PAIR):
+                    rows = slice(P * (j0 + e - GROUP * g), P * (j0 + e - GROUP * g + 1))
+                    for h in range(HALVES):
+                        nc.tensor.matmul_mx(
+                            out=acc[:, e, :],
+                            lhsT=z_codes[:, g, h, rows].bitcast(FP8X4),
+                            lhsT_scale=z_scales[:, g, h, rows],
+                            rhs=w_codes[:, h, :].bitcast(FP8X4),
+                            rhs_scale=w_scales[:, h, :],
+                            start=(h == 0),
+                            stop=(h == HALVES - 1),
+                        )
+                nc.vector.tensor_tensor(
+                    out=pre[:, j0 : j0 + PAIR, :], in0=acc[:],
+                    in1=b_all[:].unsqueeze(1).to_broadcast([P, PAIR, D]), op=ALU.add,
+                )
+                for j in range(j0, j0 + PAIR):
+                    squares = scratch.tile([P, D], F32)
+                    nc.vector.scalar_tensor_tensor(
+                        out=squares[:], in0=pre[:, j, :], scalar=0.0, in1=pre[:, j, :],
+                        op0=ALU.max, op1=ALU.mult, accum_out=sumsq[:, j : j + 1],
+                    )
+            nc.vector.tensor_scalar_max(out=norm[:, tiles], in0=sumsq[:, tiles], scalar1=1e-24)
+            nc.scalar.sqrt(out=norm[:, tiles], in_=norm[:, tiles])
+            nc.vector.reciprocal(out=rnorm[:, tiles], in_=norm[:, tiles])
+            for j in range(GROUP * g, GROUP * (g + 1)):
+                nc.scalar.activation(
+                    out=result[:, j, :], in_=pre[:, j, :], func=ACT.Relu, scale=rnorm[:, j : j + 1]
+                )
+            nc.sync.dma_start(out=out_rows[:, tiles, :], in_=result[:, tiles, :])
+
+        for g in range(GROUPS):
+            row_statistics(g)
+            normalise(g)
+            for h in range(HALVES):
+                quantise_z(g, h)
+            project(g)

@@ -62,13 +62,15 @@ def tile_textguidedcamfusion_pa_s_kernel(tc, pooled, proto, ln_g, ln_b, W, b, ou
         nc.scalar.sqrt(out=warm[:], in_=eps_col[:])
         ones = keep.tile([P, P], BF16)
         nc.vector.memset(ones[:], 1.0)
+        mean_weights = keep.tile([P, P], BF16)
+        nc.vector.memset(mean_weights[:], 1.0 / PROTOS)
         ident = keep.tile([P, P], F32)
         make_identity(nc, ident[:])
 
-        c_sum = banks.tile([P, C], F32, tag="bank")
-        nc.tensor.matmul(out=c_sum[:], lhsT=ones[:], rhs=proto_pad[:], start=True, stop=True)
+        c_bank = banks.tile([P, C], F32, tag="bank")
+        nc.tensor.matmul(out=c_bank[:], lhsT=mean_weights[:], rhs=proto_pad[:], start=True, stop=True)
         c_all = keep.tile([P, C], F32)
-        nc.scalar.activation(out=c_all[:], in_=c_sum[:], func=ACT.Copy, scale=1.0 / PROTOS)
+        nc.scalar.copy(out=c_all[:], in_=c_bank[:])
         b_sum = banks.tile([P, D], F32, tag="bank")
         nc.tensor.matmul(out=b_sum[:], lhsT=ones[:], rhs=bias_pad[:], start=True, stop=True)
         b_all = keep.tile([P, D], F32)
@@ -84,9 +86,10 @@ def tile_textguidedcamfusion_pa_s_kernel(tc, pooled, proto, ln_g, ln_b, W, b, ou
         w_codes = keep.tile([P, HALVES, D], U32, align_bytes=64)
         w_scales = keep.tile([P, HALVES, D], U8, align_bytes=64)
         for h in range(HALVES):
-            nc.scalar.copy(
+            nc.gpsimd.tensor_scalar(
                 out=w_grouped[:, h].rearrange("p (c i) t -> p c t i", i=4),
-                in_=w_raw[:, PACK * h : PACK * (h + 1), :].rearrange("p t (c i) -> p c t i", i=4),
+                in0=w_raw[:, PACK * h : PACK * (h + 1), :].rearrange("p t (c i) -> p c t i", i=4),
+                scalar1=1.0, scalar2=0.0, op0=ALU.mult, op1=ALU.add,
             )
         nc.vector.quantize_mx(
             out=w_codes[:].rearrange("p h d -> p (h d)").bitcast(FP8X4),
@@ -96,7 +99,7 @@ def tile_textguidedcamfusion_pa_s_kernel(tc, pooled, proto, ln_g, ln_b, W, b, ou
 
         stats = keep.tile([P, TILES, HALVES, STATS], F32)
         c_stats = keep.tile([P, STATS], F32)
-        nc.vector.bn_stats(out=c_stats[:], in_=c_all[:])
+        nc.vector.bn_stats(out=c_stats[:], in_=c_bank[:])
         nc.vector.tensor_copy(out=stats[:, :, 1, :], in_=c_stats[:].unsqueeze(1).to_broadcast([P, TILES, STATS]))
         mean_var = keep.tile([P, TILES, 2], F32)
         std = keep.tile([P, TILES], F32)
@@ -127,9 +130,9 @@ def tile_textguidedcamfusion_pa_s_kernel(tc, pooled, proto, ln_g, ln_b, W, b, ou
                     out=y[:, j, 0, :], in_=x[:, j, :], func=ACT.Identity,
                     scale=rstd[:, j : j + 1], bias=shift[:, j : j + 1],
                 )
-                nc.vector.tensor_scalar(
-                    out=y[:, j, 1, :], in0=c_all[:], scalar1=mean_var[:, j, 0:1], scalar2=rstd[:, j : j + 1],
-                    op0=ALU.subtract, op1=ALU.mult,
+                nc.gpsimd.tensor_scalar(
+                    out=y[:, j, 1, :], in0=c_all[:], scalar1=rstd[:, j : j + 1], scalar2=shift[:, j : j + 1],
+                    op0=ALU.mult, op1=ALU.add,
                 )
 
         def quantise_z(g, h):

@@ -126,9 +126,9 @@ def tile_textguidedcamfusion_pa_s_kernel(tc, pooled, proto, ln_g, ln_b, W, b, ou
 
         def normalise(g):
             for j in range(GROUP * g, GROUP * (g + 1)):
-                nc.scalar.activation(
-                    out=y[:, j, 0, :], in_=x[:, j, :], func=ACT.Identity,
-                    scale=rstd[:, j : j + 1], bias=shift[:, j : j + 1],
+                nc.vector.tensor_scalar(
+                    out=y[:, j, 0, :], in0=x[:, j, :], scalar1=mean_var[:, j, 0:1], scalar2=rstd[:, j : j + 1],
+                    op0=ALU.subtract, op1=ALU.mult,
                 )
                 nc.gpsimd.tensor_scalar(
                     out=y[:, j, 1, :], in0=c_all[:], scalar1=rstd[:, j : j + 1], scalar2=shift[:, j : j + 1],

@@ -16,15 +16,18 @@ PACK = 4
 ROWS = 1024
 C = 512
 HALVES = 2
+POOLED, PROTO = 0, 1
 D = 256
 PROTOS = 64
 TILES = ROWS // P
 GROUP = 2
 GROUPS = TILES // GROUP
-PAIR = 2
+GROUP_ROWS = GROUP * P
 K_BLOCKS = HALVES * PACK
+BANK_BLOCKS = 2
 STATS = 6
 EPS = 1e-5
+SKEW = 2
 FLOPS = 2 * ROWS * HALVES * C * D
 
 
@@ -33,172 +36,219 @@ def tile_textguidedcamfusion_pa_s_kernel(tc, pooled, proto, ln_g, ln_b, W, b, ou
     with ExitStack() as ctx:
         keep = ctx.enter_context(tc.tile_pool(name="keep", bufs=1))
         scratch = ctx.enter_context(tc.tile_pool(name="scratch", bufs=2))
-        banks = ctx.enter_context(tc.psum_pool(name="banks", bufs=6))
+        banks = ctx.enter_context(tc.psum_pool(name="banks", bufs=5))
         products = ctx.enter_context(tc.psum_pool(name="products", bufs=2))
 
+        gain_rows = keep.tile([P, P], BF16)
+        nc.vector.memset(gain_rows[:], 0.0)
+        bias_pad = keep.tile([P, D], BF16)
+        nc.vector.memset(bias_pad[:], 0.0)
+        proto_pad = keep.tile([P, C], BF16)
+        nc.vector.memset(proto_pad[PROTOS:P, :], 0.0)
+        nc.scalar.dma_start(out=gain_rows[0:K_BLOCKS, :], in_=ln_g.rearrange("(r c) -> r c", c=P))
+        nc.scalar.dma_start(out=gain_rows[K_BLOCKS : 2 * K_BLOCKS, :], in_=ln_b.rearrange("(r c) -> r c", c=P))
+        nc.scalar.dma_start(out=bias_pad[0:1, :], in_=b.rearrange("(o d) -> o d", o=1))
         x = keep.tile([P, TILES, C], BF16)
         pooled_rows = pooled.rearrange("(p j) c -> p j c", j=TILES)
         out_rows = out.rearrange("(p j) d -> p j d", j=TILES)
         w_raw = keep.tile([P, K_BLOCKS, D], BF16)
+        nc.sync.dma_start(out=proto_pad[0:PROTOS, :], in_=proto)
         nc.sync.dma_start(out=x[:, 0:GROUP, :], in_=pooled_rows[:, 0:GROUP, :])
         nc.sync.dma_start(out=x[:, GROUP : 2 * GROUP, :], in_=pooled_rows[:, GROUP : 2 * GROUP, :])
         nc.sync.dma_start(out=w_raw[:], in_=W.rearrange("(kb p) d -> p kb d", p=P))
         nc.sync.dma_start(out=x[:, 2 * GROUP : TILES, :], in_=pooled_rows[:, 2 * GROUP : TILES, :])
 
-        proto_pad = keep.tile([P, C], BF16)
-        nc.vector.memset(proto_pad[PROTOS:P, :], 0.0)
-        nc.scalar.dma_start(out=proto_pad[0:PROTOS, :], in_=proto)
-        gain_rows = keep.tile([P, P], BF16)
-        nc.vector.memset(gain_rows[:], 0.0)
-        nc.scalar.dma_start(out=gain_rows[0:K_BLOCKS, :], in_=ln_g.rearrange("(r c) -> r c", c=P))
-        nc.scalar.dma_start(out=gain_rows[K_BLOCKS : 2 * K_BLOCKS, :], in_=ln_b.rearrange("(r c) -> r c", c=P))
-        bias_pad = keep.tile([P, D], BF16)
-        nc.vector.memset(bias_pad[:], 0.0)
-        nc.scalar.dma_start(out=bias_pad[0:1, :], in_=b.rearrange("(o d) -> o d", o=1))
-
         eps_col = keep.tile([P, 1], F32)
         nc.vector.memset(eps_col[:], EPS)
         warm = keep.tile([P, 1], F32)
         nc.scalar.sqrt(out=warm[:], in_=eps_col[:])
-        ones = keep.tile([P, P], BF16)
-        nc.vector.memset(ones[:], 1.0)
         mean_weights = keep.tile([P, P], BF16)
         nc.vector.memset(mean_weights[:], 1.0 / PROTOS)
+        ones = keep.tile([P, P], BF16)
+        nc.vector.memset(ones[:], 1.0)
         ident = keep.tile([P, P], F32)
         make_identity(nc, ident[:])
+        gain_f32 = keep.tile([P, P], F32)
+        nc.gpsimd.tensor_copy(out=gain_f32[:], in_=gain_rows[:])
 
         c_bank = banks.tile([P, C], F32, tag="bank")
         nc.tensor.matmul(out=c_bank[:], lhsT=mean_weights[:], rhs=proto_pad[:], start=True, stop=True)
         c_all = keep.tile([P, C], F32)
         nc.scalar.copy(out=c_all[:], in_=c_bank[:])
-        b_sum = banks.tile([P, D], F32, tag="bank")
-        nc.tensor.matmul(out=b_sum[:], lhsT=ones[:], rhs=bias_pad[:], start=True, stop=True)
-        b_all = keep.tile([P, D], F32)
-        nc.scalar.copy(out=b_all[:], in_=b_sum[:])
-        gain_f32 = keep.tile([P, P], F32)
-        nc.vector.tensor_copy(out=gain_f32[:], in_=gain_rows[:])
-        gain_t = banks.tile([P, P], F32, tag="bank")
-        nc.tensor.transpose(gain_t[:], gain_f32[:], ident[:])
-        gain = keep.tile([P, 2 * K_BLOCKS], F32)
-        nc.vector.tensor_copy(out=gain[:], in_=gain_t[:, 0 : 2 * K_BLOCKS])
-
-        w_grouped = keep.tile([P, HALVES, D, PACK], BF16, align_bytes=64)
-        w_codes = keep.tile([P, HALVES, D], U32, align_bytes=64)
-        w_scales = keep.tile([P, HALVES, D], U8, align_bytes=64)
-        for h in range(HALVES):
-            nc.gpsimd.tensor_scalar(
-                out=w_grouped[:, h].rearrange("p (c i) t -> p c t i", i=4),
-                in0=w_raw[:, PACK * h : PACK * (h + 1), :].rearrange("p t (c i) -> p c t i", i=4),
-                scalar1=1.0, scalar2=0.0, op0=ALU.mult, op1=ALU.add,
-            )
-        nc.vector.quantize_mx(
-            out=w_codes[:].rearrange("p h d -> p (h d)").bitcast(FP8X4),
-            scales=w_scales[:].rearrange("p h d -> p (h d)"),
-            in_=w_grouped[:].rearrange("p h d t -> p (h d t)"),
-        )
 
         stats = keep.tile([P, TILES, HALVES, STATS], F32)
         c_stats = keep.tile([P, STATS], F32)
-        nc.vector.bn_stats(out=c_stats[:], in_=c_bank[:])
-        nc.vector.tensor_copy(out=stats[:, :, 1, :], in_=c_stats[:].unsqueeze(1).to_broadcast([P, TILES, STATS]))
         mean_var = keep.tile([P, TILES, 2], F32)
         std = keep.tile([P, TILES], F32)
         rstd = keep.tile([P, TILES], F32)
         shift = keep.tile([P, TILES], F32)
-
-        def row_statistics(g):
-            tiles = slice(GROUP * g, GROUP * (g + 1))
-            for j in range(GROUP * g, GROUP * (g + 1)):
-                nc.vector.bn_stats(out=stats[:, j, 0, :], in_=x[:, j, :])
-                nc.vector.bn_aggr(out=mean_var[:, j, :], in_=stats[:, j].rearrange("p h s -> p (h s)"))
-            nc.scalar.activation(out=std[:, tiles], in_=mean_var[:, tiles, 1], func=ACT.Sqrt, bias=eps_col[:])
-            nc.vector.reciprocal(out=rstd[:, tiles], in_=std[:, tiles])
-            nc.vector.scalar_tensor_tensor(
-                out=shift[:, tiles], in0=mean_var[:, tiles, 0], scalar=-1.0, in1=rstd[:, tiles],
-                op0=ALU.mult, op1=ALU.mult,
-            )
-
         y = keep.tile([P, TILES, HALVES, C], F32)
-        planes = keep.tile([P, GROUPS, HALVES, PACK, GROUP * P], BF16)
-        z_grouped = keep.tile([P, GROUPS, HALVES, GROUP * P, PACK], BF16, align_bytes=64)
-        z_codes = keep.tile([P, GROUPS, HALVES, GROUP * P], U32, align_bytes=64)
-        z_scales = keep.tile([P, GROUPS, HALVES, GROUP * P], U8, align_bytes=64)
-
-        def normalise(g):
-            for j in range(GROUP * g, GROUP * (g + 1)):
-                nc.vector.tensor_scalar(
-                    out=y[:, j, 0, :], in0=x[:, j, :], scalar1=mean_var[:, j, 0:1], scalar2=rstd[:, j : j + 1],
-                    op0=ALU.subtract, op1=ALU.mult,
-                )
-                nc.gpsimd.tensor_scalar(
-                    out=y[:, j, 1, :], in0=c_all[:], scalar1=rstd[:, j : j + 1], scalar2=shift[:, j : j + 1],
-                    op0=ALU.mult, op1=ALU.add,
-                )
-
-        def quantise_z(g, h):
-            for t in range(PACK):
-                kb = PACK * h + t
-                y_t = banks.tile([P, GROUP, P], F32, tag="bank")
-                for jj in range(GROUP):
-                    nc.tensor.transpose(y_t[:, jj, :], y[:, GROUP * g + jj, h, P * t : P * (t + 1)], ident[:])
-                nc.scalar.activation(
-                    out=planes[:, g, h, t, :], in_=y_t[:].rearrange("p j m -> p (j m)"), func=ACT.Identity,
-                    scale=gain[:, kb : kb + 1], bias=gain[:, K_BLOCKS + kb : K_BLOCKS + kb + 1],
-                )
-            nc.vector.tensor_copy(
-                out=z_grouped[:, g, h].rearrange("p (c i) t -> p c t i", i=4),
-                in_=planes[:, g, h].rearrange("p t (c i) -> p c t i", i=4),
-            )
-            nc.vector.quantize_mx(
-                out=z_codes[:, g, h, :].bitcast(FP8X4),
-                scales=z_scales[:, g, h, :],
-                in_=z_grouped[:, g, h].rearrange("p r t -> p (r t)"),
-            )
-
+        y_t = {}
+        gain = keep.tile([P, 2 * K_BLOCKS], F32)
+        planes = keep.tile([P, GROUPS, HALVES, PACK, GROUP_ROWS], BF16)
+        z_grouped = keep.tile([P, GROUPS, HALVES, GROUP_ROWS, PACK], BF16, align_bytes=64)
+        z_codes = keep.tile([P, GROUPS, HALVES, GROUP_ROWS], U32, align_bytes=64)
+        z_scales = keep.tile([P, GROUPS, HALVES, GROUP_ROWS], U8, align_bytes=64)
+        w_grouped = keep.tile([P, HALVES, D, PACK], BF16, align_bytes=64)
+        w_codes = keep.tile([P, HALVES, D], U32, align_bytes=64)
+        w_scales = keep.tile([P, HALVES, D], U8, align_bytes=64)
+        b_all = keep.tile([P, D], F32)
+        acc = {}
         pre = keep.tile([P, TILES, D], F32)
         sumsq = keep.tile([P, TILES], F32)
         norm = keep.tile([P, TILES], F32)
         rnorm = keep.tile([P, TILES], F32)
         result = keep.tile([P, TILES, D], F32)
 
-        def project(g):
-            tiles = slice(GROUP * g, GROUP * (g + 1))
-            for j0 in range(GROUP * g, GROUP * (g + 1), PAIR):
-                acc = products.tile([P, PAIR, D], F32)
-                for e in range(PAIR):
-                    rows = slice(P * (j0 + e - GROUP * g), P * (j0 + e - GROUP * g + 1))
-                    for h in range(HALVES):
-                        nc.tensor.matmul_mx(
-                            out=acc[:, e, :],
-                            lhsT=z_codes[:, g, h, rows].bitcast(FP8X4),
-                            lhsT_scale=z_scales[:, g, h, rows],
-                            rhs=w_codes[:, h, :].bitcast(FP8X4),
-                            rhs_scale=w_scales[:, h, :],
-                            start=(h == 0),
-                            stop=(h == HALVES - 1),
-                        )
-                nc.vector.tensor_tensor(
-                    out=pre[:, j0 : j0 + PAIR, :], in0=acc[:],
-                    in1=b_all[:].unsqueeze(1).to_broadcast([P, PAIR, D]), op=ALU.add,
-                )
-                for j in range(j0, j0 + PAIR):
-                    squares = scratch.tile([P, D], F32)
-                    nc.vector.scalar_tensor_tensor(
-                        out=squares[:], in0=pre[:, j, :], scalar=0.0, in1=pre[:, j, :],
-                        op0=ALU.max, op1=ALU.mult, accum_out=sumsq[:, j : j + 1],
-                    )
-            nc.vector.tensor_scalar_max(out=norm[:, tiles], in0=sumsq[:, tiles], scalar1=1e-24)
-            nc.scalar.sqrt(out=norm[:, tiles], in_=norm[:, tiles])
-            nc.vector.reciprocal(out=rnorm[:, tiles], in_=norm[:, tiles])
-            for j in range(GROUP * g, GROUP * (g + 1)):
-                nc.scalar.activation(
-                    out=result[:, j, :], in_=pre[:, j, :], func=ACT.Relu, scale=rnorm[:, j : j + 1]
-                )
-            nc.sync.dma_start(out=out_rows[:, tiles, :], in_=result[:, tiles, :])
+        def tiles_of(g):
+            return range(GROUP * g, GROUP * (g + 1))
 
-        for g in range(GROUPS):
-            row_statistics(g)
-            normalise(g)
+        def cols_of(g):
+            return slice(GROUP * g, GROUP * (g + 1))
+
+        def row_moments(g):
+            for j in tiles_of(g):
+                nc.vector.bn_stats(out=stats[:, j, POOLED, :], in_=x[:, j, :])
+
+        def join_moments(g):
+            for j in tiles_of(g):
+                nc.vector.bn_aggr(out=mean_var[:, j, :], in_=stats[:, j].rearrange("p h s -> p (h s)"))
+
+        def std_of(g):
+            nc.scalar.activation(out=std[:, cols_of(g)], in_=mean_var[:, cols_of(g), 1], func=ACT.Sqrt, bias=eps_col[:])
+
+        def rstd_of(g):
+            nc.vector.reciprocal(out=rstd[:, cols_of(g)], in_=std[:, cols_of(g)])
+
+        def shift_of(g):
+            nc.vector.scalar_tensor_tensor(
+                out=shift[:, cols_of(g)], in0=mean_var[:, cols_of(g), 0], scalar=-1.0, in1=rstd[:, cols_of(g)],
+                op0=ALU.mult, op1=ALU.mult,
+            )
+
+        def transpose_half(g, h):
+            for u in range(PACK // BANK_BLOCKS):
+                y_t[(g, h, u)] = banks.tile([P, BANK_BLOCKS, GROUP_ROWS], F32, tag="bank", name="y_t")
+                for v in range(BANK_BLOCKS):
+                    t = BANK_BLOCKS * u + v
+                    for e, j in enumerate(tiles_of(g)):
+                        nc.tensor.transpose(
+                            y_t[(g, h, u)][:, v, P * e : P * (e + 1)], y[:, j, h, P * t : P * (t + 1)], ident[:]
+                        )
+
+        def normalise(g):
+            for j in tiles_of(g):
+                nc.scalar.activation(
+                    out=y[:, j, POOLED, :], in_=x[:, j, :], func=ACT.Identity,
+                    scale=rstd[:, j : j + 1], bias=shift[:, j : j + 1],
+                )
+                nc.vector.tensor_scalar(
+                    out=y[:, j, PROTO, :], in0=c_all[:], scalar1=rstd[:, j : j + 1], scalar2=shift[:, j : j + 1],
+                    op0=ALU.mult, op1=ALU.add,
+                )
+
+        def transpose(g):
             for h in range(HALVES):
-                quantise_z(g, h)
-            project(g)
+                transpose_half(g, h)
+
+        def gain_and_shift(g):
+            for kb in range(K_BLOCKS):
+                h, t = divmod(kb, PACK)
+                nc.scalar.activation(
+                    out=planes[:, g, h, t, :], in_=y_t[(g, h, t // BANK_BLOCKS)][:, t % BANK_BLOCKS, :],
+                    func=ACT.Identity, scale=gain[:, kb : kb + 1], bias=gain[:, K_BLOCKS + kb : K_BLOCKS + kb + 1],
+                )
+
+        def regroup(g):
+            for h in range(HALVES):
+                nc.vector.tensor_copy(
+                    out=z_grouped[:, g, h].rearrange("p (c i) t -> p c t i", i=4),
+                    in_=planes[:, g, h].rearrange("p t (c i) -> p c t i", i=4),
+                )
+
+        def quantise(g):
+            for h in range(HALVES):
+                nc.vector.quantize_mx(
+                    out=z_codes[:, g, h, :].bitcast(FP8X4),
+                    scales=z_scales[:, g, h, :],
+                    in_=z_grouped[:, g, h].rearrange("p r t -> p (r t)"),
+                )
+
+        def regroup_w(h):
+            nc.gpsimd.tensor_scalar(
+                out=w_grouped[:, h].rearrange("p (c i) t -> p c t i", i=4),
+                in0=w_raw[:, PACK * h : PACK * (h + 1), :].rearrange("p t (c i) -> p c t i", i=4),
+                scalar1=1.0, scalar2=0.0, op0=ALU.mult, op1=ALU.add,
+            )
+
+        def quantise_w():
+            nc.vector.quantize_mx(
+                out=w_codes[:].rearrange("p h d -> p (h d)").bitcast(FP8X4),
+                scales=w_scales[:].rearrange("p h d -> p (h d)"),
+                in_=w_grouped[:].rearrange("p h d t -> p (h d t)"),
+            )
+
+        def project(g):
+            acc[g] = products.tile([P, GROUP, D], F32, name="acc")
+            for e in range(GROUP):
+                rows = slice(P * e, P * (e + 1))
+                for h in range(HALVES):
+                    nc.tensor.matmul_mx(
+                        out=acc[g][:, e, :],
+                        lhsT=z_codes[:, g, h, rows].bitcast(FP8X4),
+                        lhsT_scale=z_scales[:, g, h, rows],
+                        rhs=w_codes[:, h, :].bitcast(FP8X4),
+                        rhs_scale=w_scales[:, h, :],
+                        start=(h == 0),
+                        stop=(h == HALVES - 1),
+                    )
+
+        def add_bias(g):
+            nc.vector.tensor_tensor(
+                out=pre[:, cols_of(g), :], in0=acc[g][:],
+                in1=b_all[:].unsqueeze(1).to_broadcast([P, GROUP, D]), op=ALU.add,
+            )
+
+        def sum_squares(g):
+            for j in tiles_of(g):
+                squares = scratch.tile([P, D], F32)
+                nc.vector.scalar_tensor_tensor(
+                    out=squares[:], in0=pre[:, j, :], scalar=0.0, in1=pre[:, j, :],
+                    op0=ALU.max, op1=ALU.mult, accum_out=sumsq[:, j : j + 1],
+                )
+
+        def floor_sumsq(g):
+            nc.vector.tensor_scalar_max(out=norm[:, cols_of(g)], in0=sumsq[:, cols_of(g)], scalar1=1e-24)
+
+        def norm_of(g):
+            nc.scalar.sqrt(out=norm[:, cols_of(g)], in_=norm[:, cols_of(g)])
+
+        def rnorm_of(g):
+            nc.vector.reciprocal(out=rnorm[:, cols_of(g)], in_=norm[:, cols_of(g)])
+
+        def scale_and_store(g):
+            for j in tiles_of(g):
+                nc.scalar.activation(out=result[:, j, :], in_=pre[:, j, :], func=ACT.Relu, scale=rnorm[:, j : j + 1])
+            nc.sync.dma_start(out=out_rows[:, cols_of(g), :], in_=result[:, cols_of(g), :])
+
+        nc.vector.bn_stats(out=c_stats[:], in_=c_bank[:])
+        nc.vector.tensor_copy(out=stats[:, :, PROTO, :], in_=c_stats[:].unsqueeze(1).to_broadcast([P, TILES, STATS]))
+        b_bank = banks.tile([P, D], F32, tag="bank")
+        nc.tensor.matmul(out=b_bank[:], lhsT=ones[:], rhs=bias_pad[:], start=True, stop=True)
+        gain_t = banks.tile([P, P], F32, tag="bank")
+        nc.tensor.transpose(gain_t[:], gain_f32[:], ident[:])
+        nc.scalar.copy(out=gain[:], in_=gain_t[:, 0 : 2 * K_BLOCKS])
+        nc.scalar.copy(out=b_all[:], in_=b_bank[:])
+        for h in range(HALVES):
+            regroup_w(h)
+        quantise_w()
+
+        stages = [
+            row_moments, join_moments, std_of, rstd_of, shift_of, normalise, transpose, gain_and_shift, regroup,
+            quantise, project, add_bias, sum_squares, floor_sumsq, norm_of, rnorm_of, scale_and_store,
+        ]
+        for wave in range(len(stages) + SKEW * (GROUPS - 1)):
+            for g in range(GROUPS):
+                s = wave - SKEW * g
+                if 0 <= s < len(stages):
+                    stages[s](g)

from contextlib import ExitStack

import concourse.mybir as mybir
from concourse.masks import make_identity

F32 = mybir.dt.float32
BF16 = mybir.dt.bfloat16
U32 = mybir.dt.uint32
U8 = mybir.dt.uint8
FP8X4 = mybir.dt.float8_e4m3fn_x4
ALU = mybir.AluOpType
ACT = mybir.ActivationFunctionType

P = 128
PACK = 4
ROWS = 1024
C = 512
HALVES = 2
POOLED, PROTO = 0, 1
D = 256
PROTOS = 64
TILES = ROWS // P
GROUP = 2
GROUPS = TILES // GROUP
GROUP_ROWS = GROUP * P
K_BLOCKS = HALVES * PACK
BANK_BLOCKS = 2
STATS = 6
EPS = 1e-5
SKEW = 2
FLOPS = 2 * ROWS * HALVES * C * D


def tile_textguidedcamfusion_pa_s_kernel(tc, pooled, proto, ln_g, ln_b, W, b, out):
    nc = tc.nc
    with ExitStack() as ctx:
        keep = ctx.enter_context(tc.tile_pool(name="keep", bufs=1))
        scratch = ctx.enter_context(tc.tile_pool(name="scratch", bufs=2))
        banks = ctx.enter_context(tc.psum_pool(name="banks", bufs=5))
        products = ctx.enter_context(tc.psum_pool(name="products", bufs=2))

        gain_rows = keep.tile([P, P], BF16)
        nc.vector.memset(gain_rows[:], 0.0)
        bias_pad = keep.tile([P, D], BF16)
        nc.vector.memset(bias_pad[:], 0.0)
        proto_pad = keep.tile([P, C], BF16)
        nc.vector.memset(proto_pad[PROTOS:P, :], 0.0)
        nc.scalar.dma_start(out=gain_rows[0:K_BLOCKS, :], in_=ln_g.rearrange("(r c) -> r c", c=P))
        nc.scalar.dma_start(out=gain_rows[K_BLOCKS : 2 * K_BLOCKS, :], in_=ln_b.rearrange("(r c) -> r c", c=P))
        nc.scalar.dma_start(out=bias_pad[0:1, :], in_=b.rearrange("(o d) -> o d", o=1))
        x = keep.tile([P, TILES, C], BF16)
        pooled_rows = pooled.rearrange("(p j) c -> p j c", j=TILES)
        out_rows = out.rearrange("(p j) d -> p j d", j=TILES)
        w_raw = keep.tile([P, K_BLOCKS, D], BF16)
        nc.sync.dma_start(out=proto_pad[0:PROTOS, :], in_=proto)
        nc.sync.dma_start(out=x[:, 0:GROUP, :], in_=pooled_rows[:, 0:GROUP, :])
        nc.sync.dma_start(out=x[:, GROUP : 2 * GROUP, :], in_=pooled_rows[:, GROUP : 2 * GROUP, :])
        nc.sync.dma_start(out=w_raw[:], in_=W.rearrange("(kb p) d -> p kb d", p=P))
        nc.sync.dma_start(out=x[:, 2 * GROUP : TILES, :], in_=pooled_rows[:, 2 * GROUP : TILES, :])

        eps_col = keep.tile([P, 1], F32)
        nc.vector.memset(eps_col[:], EPS)
        warm = keep.tile([P, 1], F32)
        nc.scalar.sqrt(out=warm[:], in_=eps_col[:])
        mean_weights = keep.tile([P, P], BF16)
        nc.vector.memset(mean_weights[:], 1.0 / PROTOS)
        ones = keep.tile([P, P], BF16)
        nc.vector.memset(ones[:], 1.0)
        ident = keep.tile([P, P], F32)
        make_identity(nc, ident[:])
        gain_f32 = keep.tile([P, P], F32)
        nc.gpsimd.tensor_copy(out=gain_f32[:], in_=gain_rows[:])

        c_bank = banks.tile([P, C], F32, tag="bank")
        nc.tensor.matmul(out=c_bank[:], lhsT=mean_weights[:], rhs=proto_pad[:], start=True, stop=True)
        c_all = keep.tile([P, C], F32)
        nc.scalar.copy(out=c_all[:], in_=c_bank[:])

        stats = keep.tile([P, TILES, HALVES, STATS], F32)
        c_stats = keep.tile([P, STATS], F32)
        mean_var = keep.tile([P, TILES, 2], F32)
        std = keep.tile([P, TILES], F32)
        rstd = keep.tile([P, TILES], F32)
        shift = keep.tile([P, TILES], F32)
        y = keep.tile([P, TILES, HALVES, C], F32)
        y_t = {}
        gain = keep.tile([P, 2 * K_BLOCKS], F32)
        planes = keep.tile([P, GROUPS, HALVES, PACK, GROUP_ROWS], BF16)
        z_grouped = keep.tile([P, GROUPS, HALVES, GROUP_ROWS, PACK], BF16, align_bytes=64)
        z_codes = keep.tile([P, GROUPS, HALVES, GROUP_ROWS], U32, align_bytes=64)
        z_scales = keep.tile([P, GROUPS, HALVES, GROUP_ROWS], U8, align_bytes=64)
        w_grouped = keep.tile([P, HALVES, D, PACK], BF16, align_bytes=64)
        w_codes = keep.tile([P, HALVES, D], U32, align_bytes=64)
        w_scales = keep.tile([P, HALVES, D], U8, align_bytes=64)
        b_all = keep.tile([P, D], F32)
        acc = {}
        pre = keep.tile([P, TILES, D], F32)
        sumsq = keep.tile([P, TILES], F32)
        norm = keep.tile([P, TILES], F32)
        rnorm = keep.tile([P, TILES], F32)
        result = keep.tile([P, TILES, D], F32)

        def tiles_of(g):
            return range(GROUP * g, GROUP * (g + 1))

        def cols_of(g):
            return slice(GROUP * g, GROUP * (g + 1))

        def row_moments(g):
            for j in tiles_of(g):
                nc.vector.bn_stats(out=stats[:, j, POOLED, :], in_=x[:, j, :])

        def join_moments(g):
            for j in tiles_of(g):
                nc.vector.bn_aggr(out=mean_var[:, j, :], in_=stats[:, j].rearrange("p h s -> p (h s)"))

        def std_of(g):
            nc.scalar.activation(out=std[:, cols_of(g)], in_=mean_var[:, cols_of(g), 1], func=ACT.Sqrt, bias=eps_col[:])

        def rstd_of(g):
            nc.vector.reciprocal(out=rstd[:, cols_of(g)], in_=std[:, cols_of(g)])

        def shift_of(g):
            nc.vector.scalar_tensor_tensor(
                out=shift[:, cols_of(g)], in0=mean_var[:, cols_of(g), 0], scalar=-1.0, in1=rstd[:, cols_of(g)],
                op0=ALU.mult, op1=ALU.mult,
            )

        def transpose_half(g, h):
            for u in range(PACK // BANK_BLOCKS):
                y_t[(g, h, u)] = banks.tile([P, BANK_BLOCKS, GROUP_ROWS], F32, tag="bank", name="y_t")
                for v in range(BANK_BLOCKS):
                    t = BANK_BLOCKS * u + v
                    for e, j in enumerate(tiles_of(g)):
                        nc.tensor.transpose(
                            y_t[(g, h, u)][:, v, P * e : P * (e + 1)], y[:, j, h, P * t : P * (t + 1)], ident[:]
                        )

        def normalise(g):
            for j in tiles_of(g):
                nc.scalar.activation(
                    out=y[:, j, POOLED, :], in_=x[:, j, :], func=ACT.Identity,
                    scale=rstd[:, j : j + 1], bias=shift[:, j : j + 1],
                )
                nc.vector.tensor_scalar(
                    out=y[:, j, PROTO, :], in0=c_all[:], scalar1=rstd[:, j : j + 1], scalar2=shift[:, j : j + 1],
                    op0=ALU.mult, op1=ALU.add,
                )

        def transpose(g):
            for h in range(HALVES):
                transpose_half(g, h)

        def gain_and_shift(g):
            for kb in range(K_BLOCKS):
                h, t = divmod(kb, PACK)
                nc.scalar.activation(
                    out=planes[:, g, h, t, :], in_=y_t[(g, h, t // BANK_BLOCKS)][:, t % BANK_BLOCKS, :],
                    func=ACT.Identity, scale=gain[:, kb : kb + 1], bias=gain[:, K_BLOCKS + kb : K_BLOCKS + kb + 1],
                )

        def regroup(g):
            for h in range(HALVES):
                nc.vector.tensor_copy(
                    out=z_grouped[:, g, h].rearrange("p (c i) t -> p c t i", i=4),
                    in_=planes[:, g, h].rearrange("p t (c i) -> p c t i", i=4),
                )

        def quantise(g):
            for h in range(HALVES):
                nc.vector.quantize_mx(
                    out=z_codes[:, g, h, :].bitcast(FP8X4),
                    scales=z_scales[:, g, h, :],
                    in_=z_grouped[:, g, h].rearrange("p r t -> p (r t)"),
                )

        def regroup_w(h):
            nc.gpsimd.tensor_scalar(
                out=w_grouped[:, h].rearrange("p (c i) t -> p c t i", i=4),
                in0=w_raw[:, PACK * h : PACK * (h + 1), :].rearrange("p t (c i) -> p c t i", i=4),
                scalar1=1.0, scalar2=0.0, op0=ALU.mult, op1=ALU.add,
            )

        def quantise_w():
            nc.vector.quantize_mx(
                out=w_codes[:].rearrange("p h d -> p (h d)").bitcast(FP8X4),
                scales=w_scales[:].rearrange("p h d -> p (h d)"),
                in_=w_grouped[:].rearrange("p h d t -> p (h d t)"),
            )

        def project(g):
            acc[g] = products.tile([P, GROUP, D], F32, name="acc")
            for e in range(GROUP):
                rows = slice(P * e, P * (e + 1))
                for h in range(HALVES):
                    nc.tensor.matmul_mx(
                        out=acc[g][:, e, :],
                        lhsT=z_codes[:, g, h, rows].bitcast(FP8X4),
                        lhsT_scale=z_scales[:, g, h, rows],
                        rhs=w_codes[:, h, :].bitcast(FP8X4),
                        rhs_scale=w_scales[:, h, :],
                        start=(h == 0),
                        stop=(h == HALVES - 1),
                    )

        def add_bias(g):
            nc.vector.tensor_tensor(
                out=pre[:, cols_of(g), :], in0=acc[g][:],
                in1=b_all[:].unsqueeze(1).to_broadcast([P, GROUP, D]), op=ALU.add,
            )

        def sum_squares(g):
            for j in tiles_of(g):
                squares = scratch.tile([P, D], F32)
                nc.vector.scalar_tensor_tensor(
                    out=squares[:], in0=pre[:, j, :], scalar=0.0, in1=pre[:, j, :],
                    op0=ALU.max, op1=ALU.mult, accum_out=sumsq[:, j : j + 1],
                )

        def floor_sumsq(g):
            nc.vector.tensor_scalar_max(out=norm[:, cols_of(g)], in0=sumsq[:, cols_of(g)], scalar1=1e-24)

        def norm_of(g):
            nc.scalar.sqrt(out=norm[:, cols_of(g)], in_=norm[:, cols_of(g)])

        def rnorm_of(g):
            nc.vector.reciprocal(out=rnorm[:, cols_of(g)], in_=norm[:, cols_of(g)])

        def scale_and_store(g):
            for j in tiles_of(g):
                nc.scalar.activation(out=result[:, j, :], in_=pre[:, j, :], func=ACT.Relu, scale=rnorm[:, j : j + 1])
            nc.sync.dma_start(out=out_rows[:, cols_of(g), :], in_=result[:, cols_of(g), :])

        nc.vector.bn_stats(out=c_stats[:], in_=c_bank[:])
        nc.vector.tensor_copy(out=stats[:, :, PROTO, :], in_=c_stats[:].unsqueeze(1).to_broadcast([P, TILES, STATS]))
        b_bank = banks.tile([P, D], F32, tag="bank")
        nc.tensor.matmul(out=b_bank[:], lhsT=ones[:], rhs=bias_pad[:], start=True, stop=True)
        gain_t = banks.tile([P, P], F32, tag="bank")
        nc.tensor.transpose(gain_t[:], gain_f32[:], ident[:])
        nc.scalar.copy(out=gain[:], in_=gain_t[:, 0 : 2 * K_BLOCKS])
        nc.scalar.copy(out=b_all[:], in_=b_bank[:])
        for h in range(HALVES):
            regroup_w(h)
        quantise_w()

        stages = [
            row_moments, join_moments, std_of, rstd_of, shift_of, normalise, transpose, gain_and_shift, regroup,
            quantise, project, add_bias, sum_squares, floor_sumsq, norm_of, rnorm_of, scale_and_store,
        ]
        for wave in range(len(stages) + SKEW * (GROUPS - 1)):
            for g in range(GROUPS):
                s = wave - SKEW * g
                if 0 <= s < len(stages):
                    stages[s](g)
